import numpy as np
import ml_dtypes

BF16 = ml_dtypes.bfloat16


def bf(x):
    return np.asarray(x, np.float32).astype(BF16)


def f32(x):
    return np.asarray(x, np.float32)


def f64(x):
    return np.asarray(x).astype(np.float64)


def striped(idx):
    return np.tile(idx.reshape(-1, 16).T, (8, 1))


S, D, M, H, K, N = 256, 128, 256, 128, 8, 1024
A = 0.25


def prelu(v):
    return np.where(v >= 0.0, v, A * v)


def setup_inputs():
    return {"table": bf(np.random.standard_normal((D, S))), "w": bf(np.random.standard_normal((D, M)) / np.sqrt(D)), "b": f32(0.1 * np.random.standard_normal((M, 1))), "offs": striped(np.concatenate([np.random.permutation(S)[:H] for _ in range(K)]))}


def reference(table, w, b, offs):
    idx = offs[:16].T.reshape(-1)
    p = f64(w).T @ f64(table)[:, idx]
    return prelu(p.reshape(M, K, H).sum(axis=1) / K + f64(b))

@@ -1,0 +1,51 @@
+import concourse.mybir as mybir
+
+BF16, F32, U16 = mybir.dt.bfloat16, mybir.dt.float32, mybir.dt.uint16
+MULT, ADD, MAX = mybir.AluOpType.mult, mybir.AluOpType.add, mybir.AluOpType.max
+
+P = 128
+U_NODES = 256
+HIDDEN = 256
+V_NODES = 128
+NEIGHBOURS = 8
+LIST = NEIGHBOURS * V_NODES
+PIECE_COLUMNS = V_NODES // 16
+SLOPE = 0.25
+
+FLOPS = 2 * P * HIDDEN * LIST
+
+
+def tile_modeler_kernel(tc, table, w, b, offs, out):
+    nc = tc.nc
+    blocks = HIDDEN // P
+    with (
+        tc.tile_pool(name="held", bufs=1) as held,
+        tc.tile_pool(name="work", bufs=2) as work,
+        tc.psum_pool(name="psum", bufs=2) as psum,
+    ):
+        offsets = held.tile([P, LIST // 16], U16, name="offsets")
+        nc.sync.dma_start(offsets[:], offs)
+        features = held.tile([P, U_NODES], BF16, name="features")
+        nc.scalar.dma_start(features[:], table)
+        weights = held.tile([P, HIDDEN], BF16, name="weights")
+        nc.sync.dma_start(weights[:], w)
+        bias = held.tile([P, blocks], F32, name="bias")
+        with nc.allow_non_contiguous_dma(reason="256 bias values, one to a partition"):
+            nc.scalar.dma_start(bias[:], b.rearrange("(i p) o -> p (i o)", p=P))
+
+        for i in range(blocks):
+            total = psum.tile([P, V_NODES], F32, name="total")
+            for t in range(NEIGHBOURS):
+                piece = offsets[:, t * PIECE_COLUMNS : (t + 1) * PIECE_COLUMNS]
+                nc.tensor.matmul(
+                    total[:],
+                    weights[:, i * P : (i + 1) * P],
+                    features[:].indirect(piece),
+                    start=(t == 0),
+                    stop=(t == NEIGHBOURS - 1),
+                )
+            y = work.tile([P, V_NODES], F32, name="y")
+            nc.vector.tensor_scalar(y[:], total[:], 1.0 / NEIGHBOURS, bias[:, i : i + 1], MULT, ADD)
+            result = work.tile([P, V_NODES], F32, name="result")
+            nc.vector.scalar_tensor_tensor(result[:], y[:], SLOPE, y[:], MULT, MAX)
+            nc.sync.dma_start(out[i * P : (i + 1) * P, :], result[:])

@@ -27,8 +27,9 @@ def tile_modeler_kernel(tc, table, w, b, offs, out):
         nc.sync.dma_start(offsets[:], offs)
         features = held.tile([P, U_NODES], BF16, name="features")
         nc.scalar.dma_start(features[:], table)
-        weights = held.tile([P, HIDDEN], BF16, name="weights")
-        nc.sync.dma_start(weights[:], w)
+        weights = [held.tile([P, P], BF16, name="weights%d" % i) for i in range(blocks)]
+        nc.sync.dma_start(weights[0][:], w[:, :P])
+        nc.scalar.dma_start(weights[1][:], w[:, P:])
         bias = held.tile([P, blocks], F32, name="bias")
         with nc.allow_non_contiguous_dma(reason="256 bias values, one to a partition"):
             nc.scalar.dma_start(bias[:], b.rearrange("(i p) o -> p (i o)", p=P))
@@ -39,7 +40,7 @@ def tile_modeler_kernel(tc, table, w, b, offs, out):
                 piece = offsets[:, t * PIECE_COLUMNS : (t + 1) * PIECE_COLUMNS]
                 nc.tensor.matmul(
                     total[:],
-                    weights[:, i * P : (i + 1) * P],
+                    weights[i][:],
                     features[:].indirect(piece),
                     start=(t == 0),
                     stop=(t == NEIGHBOURS - 1),

@@ -9,8 +9,13 @@ HIDDEN = 256
 V_NODES = 128
 NEIGHBOURS = 8
 LIST = NEIGHBOURS * V_NODES
-PIECE_COLUMNS = V_NODES // 16
+NARROW_COLUMNS = V_NODES // 16
 SLOPE = 0.25
+MEAN = 1.0 / NEIGHBOURS
+
+WIDE_PIECES = 2
+WIDE_COLUMNS = 2 * NARROW_COLUMNS
+FIRST_NARROW = 2 * WIDE_PIECES
 
 FLOPS = 2 * P * HIDDEN * LIST
 
@@ -34,19 +39,37 @@ def tile_modeler_kernel(tc, table, w, b, offs, out):
         with nc.allow_non_contiguous_dma(reason="256 bias values, one to a partition"):
             nc.scalar.dma_start(bias[:], b.rearrange("(i p) o -> p (i o)", p=P))
 
+        early = []
         for i in range(blocks):
-            total = psum.tile([P, V_NODES], F32, name="total")
-            for t in range(NEIGHBOURS):
-                piece = offsets[:, t * PIECE_COLUMNS : (t + 1) * PIECE_COLUMNS]
+            wide = psum.tile([P, 2 * V_NODES], F32, name="wide")
+            for u in range(WIDE_PIECES):
+                piece = offsets[:, u * WIDE_COLUMNS : (u + 1) * WIDE_COLUMNS]
                 nc.tensor.matmul(
-                    total[:],
+                    wide[:],
                     weights[i][:],
                     features[:].indirect(piece),
-                    start=(t == 0),
+                    start=(u == 0),
+                    stop=(u == WIDE_PIECES - 1),
+                )
+            even = work.tile([P, V_NODES], F32, name="even")
+            nc.vector.tensor_scalar(even[:], wide[:, :V_NODES], MEAN, bias[:, i : i + 1], MULT, ADD)
+            both = work.tile([P, V_NODES], F32, name="both")
+            nc.vector.scalar_tensor_tensor(both[:], wide[:, V_NODES:], MEAN, even[:], MULT, ADD)
+            early.append(both)
+
+        for i in range(blocks):
+            narrow = psum.tile([P, V_NODES], F32, name="narrow")
+            for t in range(FIRST_NARROW, NEIGHBOURS):
+                piece = offsets[:, t * NARROW_COLUMNS : (t + 1) * NARROW_COLUMNS]
+                nc.tensor.matmul(
+                    narrow[:],
+                    weights[i][:],
+                    features[:].indirect(piece),
+                    start=(t == FIRST_NARROW),
                     stop=(t == NEIGHBOURS - 1),
                 )
             y = work.tile([P, V_NODES], F32, name="y")
-            nc.vector.tensor_scalar(y[:], total[:], 1.0 / NEIGHBOURS, bias[:, i : i + 1], MULT, ADD)
+            nc.vector.scalar_tensor_tensor(y[:], narrow[:], MEAN, early[i][:], MULT, ADD)
             result = work.tile([P, V_NODES], F32, name="result")
             nc.vector.scalar_tensor_tensor(result[:], y[:], SLOPE, y[:], MULT, MAX)
             nc.sync.dma_start(out[i * P : (i + 1) * P, :], result[:])

import concourse.mybir as mybir

BF16, F32, U16 = mybir.dt.bfloat16, mybir.dt.float32, mybir.dt.uint16
MULT, ADD, MAX = mybir.AluOpType.mult, mybir.AluOpType.add, mybir.AluOpType.max

P = 128
U_NODES = 256
HIDDEN = 256
V_NODES = 128
NEIGHBOURS = 8
LIST = NEIGHBOURS * V_NODES
NARROW_COLUMNS = V_NODES // 16
SLOPE = 0.25
MEAN = 1.0 / NEIGHBOURS

WIDE_PIECES = 2
WIDE_COLUMNS = 2 * NARROW_COLUMNS
FIRST_NARROW = 2 * WIDE_PIECES

FLOPS = 2 * P * HIDDEN * LIST


def tile_modeler_kernel(tc, table, w, b, offs, out):
    nc = tc.nc
    blocks = HIDDEN // P
    with (
        tc.tile_pool(name="held", bufs=1) as held,
        tc.tile_pool(name="work", bufs=2) as work,
        tc.psum_pool(name="psum", bufs=2) as psum,
    ):
        offsets = held.tile([P, LIST // 16], U16, name="offsets")
        nc.sync.dma_start(offsets[:], offs)
        features = held.tile([P, U_NODES], BF16, name="features")
        nc.scalar.dma_start(features[:], table)
        weights = [held.tile([P, P], BF16, name="weights%d" % i) for i in range(blocks)]
        nc.sync.dma_start(weights[0][:], w[:, :P])
        nc.scalar.dma_start(weights[1][:], w[:, P:])
        bias = held.tile([P, blocks], F32, name="bias")
        with nc.allow_non_contiguous_dma(reason="256 bias values, one to a partition"):
            nc.scalar.dma_start(bias[:], b.rearrange("(i p) o -> p (i o)", p=P))

        early = []
        for i in range(blocks):
            wide = psum.tile([P, 2 * V_NODES], F32, name="wide")
            for u in range(WIDE_PIECES):
                piece = offsets[:, u * WIDE_COLUMNS : (u + 1) * WIDE_COLUMNS]
                nc.tensor.matmul(
                    wide[:],
                    weights[i][:],
                    features[:].indirect(piece),
                    start=(u == 0),
                    stop=(u == WIDE_PIECES - 1),
                )
            even = work.tile([P, V_NODES], F32, name="even")
            nc.vector.tensor_scalar(even[:], wide[:, :V_NODES], MEAN, bias[:, i : i + 1], MULT, ADD)
            both = work.tile([P, V_NODES], F32, name="both")
            nc.vector.scalar_tensor_tensor(both[:], wide[:, V_NODES:], MEAN, even[:], MULT, ADD)
            early.append(both)

        for i in range(blocks):
            narrow = psum.tile([P, V_NODES], F32, name="narrow")
            for t in range(FIRST_NARROW, NEIGHBOURS):
                piece = offsets[:, t * NARROW_COLUMNS : (t + 1) * NARROW_COLUMNS]
                nc.tensor.matmul(
                    narrow[:],
                    weights[i][:],
                    features[:].indirect(piece),
                    start=(t == FIRST_NARROW),
                    stop=(t == NEIGHBOURS - 1),
                )
            y = work.tile([P, V_NODES], F32, name="y")
            nc.vector.scalar_tensor_tensor(y[:], narrow[:], MEAN, early[i][:], MULT, ADD)
            result = work.tile([P, V_NODES], F32, name="result")
            nc.vector.scalar_tensor_tensor(result[:], y[:], SLOPE, y[:], MULT, MAX)
            nc.sync.dma_start(out[i * P : (i + 1) * P, :], result[:])
